import numpy as np
import ml_dtypes


def mxq(x, axis, fmt="e4m3"):
    dtype, down = {"e4m3": (ml_dtypes.float8_e4m3fn, 7), "e5m2": (ml_dtypes.float8_e5m2, 14)}[fmt]
    v = np.moveaxis(np.asarray(x, np.float32).astype(ml_dtypes.bfloat16).astype(np.float64), axis, -1)
    blocks = v.reshape(v.shape[:-1] + (-1, 32))
    amax = np.abs(blocks).max(-1, keepdims=True)
    byte = np.maximum(np.where(amax > 0, np.frexp(amax)[1] - 1 + 127, 0) - down, 1)
    scale = np.exp2(byte - 127.0)
    codes = (blocks / scale).astype(np.float32).astype(dtype).astype(np.float64)
    return np.moveaxis((codes * scale).reshape(v.shape), -1, axis)


WIDE = False


def mx_kscale(k):
    if not WIDE:
        return np.ones(k)
    levels = np.array([10, -10, 5, -5, 0])
    if k % 512:
        return np.exp2(np.random.permutation(np.resize(levels, k // 32))).repeat(32)
    a = np.empty((k // 512, 16))
    for p in range(k // 512):
        a[p, :8] = np.random.permutation(np.resize(levels, 8))
        for g in range(8):
            far = levels[np.abs(levels - a[p, g]) >= 10]
            a[p, g + 8] = far[np.random.randint(len(far))]
    return np.exp2(a.ravel()).repeat(32)


BF16 = ml_dtypes.bfloat16


def bf(x):
    return np.asarray(x, np.float32).astype(BF16)


def f64(x):
    return np.asarray(x).astype(np.float64)


B, S, D, N = 4, 64, 2048, 2048
EPS = 1e-6
GS = 6.0 / np.sqrt(D)
LEVELS = np.array([-1.0, -0.5, 0.0, 0.5, 1.0])
PROBS = np.array([0.23, 0.17, 0.2, 0.17, 0.23])


def setup_inputs():
    s = mx_kscale(D)
    s2 = np.concatenate([s, s])
    return {"x_real": bf(np.random.standard_normal((B, S, D)) * 1.2 + 0.5),
            "x_imag": bf(np.random.standard_normal((B, S, D)) * 0.7 + 0.1),
            "qw_re": bf(np.random.choice(LEVELS, size=(N, D), p=PROBS) / s),
            "qw_im": bf(np.random.choice(LEVELS, size=(N, D), p=PROBS) / s),
            "gamma": bf((1.0 + 0.1 * np.random.standard_normal(D + D)) * GS * s2),
            "beta": bf(0.2 * np.random.standard_normal(D + D) * GS * s2),
            "s_re": bf(0.7 + 0.05 * np.random.standard_normal(1)),
            "s_im": bf(0.9 + 0.05 * np.random.standard_normal(1))}


def reference(x_real, x_imag, qw_re, qw_im, gamma, beta, s_re, s_im):
    x_cat = np.concatenate([f64(x_real), f64(x_imag)], axis=-1)
    mu = x_cat.mean(axis=-1, keepdims=True)
    var = x_cat.var(axis=-1, keepdims=True)
    norm = (x_cat - mu) * (1.0 / np.sqrt(var + EPS)) * f64(gamma) + f64(beta)
    nr = mxq(norm[..., :D], 2, "e4m3")
    ni = mxq(norm[..., D:], 2, "e4m3")
    wr = mxq(f64(qw_re), 1, "e4m3").T
    wi = mxq(f64(qw_im), 1, "e4m3").T
    y_real = (nr @ wr) - (ni @ wi)
    y_imag = (nr @ wi) + (ni @ wr)
    return y_real * f64(s_re), y_imag * f64(s_im)

@@ -1,0 +1,302 @@
+from contextlib import ExitStack
+
+import concourse.mybir as mybir
+from concourse.masks import make_identity
+
+F32 = mybir.dt.float32
+BF16 = mybir.dt.bfloat16
+U32 = mybir.dt.uint32
+U8 = mybir.dt.uint8
+FP8X4 = mybir.dt.float8_e4m3fn_x4
+ALU = mybir.AluOpType
+ACT = mybir.ActivationFunctionType
+
+P = 128
+TOKENS = 256
+TOKEN_TILES = TOKENS // P
+D = 2048
+N_OUT = 2048
+EPS = 1e-6
+
+REAL, IMAG = 0, 1
+NR, NI, NEG_NI = 0, 1, 2
+
+PACK = 4
+K_PASS = P * PACK
+PASSES = D // K_PASS
+PIECES = 2 * PASSES
+N_CHUNK = 256
+ROUNDS = N_OUT // N_CHUNK
+CHUNKS = 2 * ROUNDS
+STEPS = 2 * ROUNDS
+ACC_COLS = 2 * N_CHUNK
+BN_COLS = 512
+BN_PARTS = 2 * D // BN_COLS
+GB_COLS = K_PASS
+GB_ROWS = 2 * D // GB_COLS
+
+W_BUFS = 5
+T_LEAD = 4
+Q_LEAD = T_LEAD - 1
+X1_AFTER_CHUNK = 5
+STATS_STEPS = 4
+PIECE_STEP = STATS_STEPS + 1
+
+FLOPS = 4 * 2 * TOKENS * D * N_OUT
+
+
+def tile_realimagfourvallinear_pa_kernel(
+    tc, x_real, x_imag, qw_re, qw_im, gamma, beta, s_re, s_im, out_0, out_1
+):
+    nc = tc.nc
+    x_streams = (x_real.flatten_outer_dims(), x_imag.flatten_outer_dims())
+    weights = (qw_re, qw_im)
+    outs = (out_0.flatten_outer_dims(), out_1.flatten_outer_dims())
+
+    with ExitStack() as ctx:
+        const = ctx.enter_context(tc.tile_pool(name="const", bufs=1))
+        keep = ctx.enter_context(tc.tile_pool(name="keep", bufs=1))
+        small = ctx.enter_context(tc.tile_pool(name="small", bufs=2))
+        w_pool = ctx.enter_context(tc.tile_pool(name="w_pool", bufs=W_BUFS))
+        wg_pool = ctx.enter_context(tc.tile_pool(name="wg_pool", bufs=3))
+        z_pool = ctx.enter_context(tc.tile_pool(name="z_pool", bufs=PIECES))
+        planes_pool = ctx.enter_context(tc.tile_pool(name="planes_pool", bufs=2))
+        xg_pool = ctx.enter_context(tc.tile_pool(name="xg_pool", bufs=3))
+        y_pool = ctx.enter_context(tc.tile_pool(name="y_pool", bufs=4))
+        wt_psum = ctx.enter_context(tc.psum_pool(name="wt_psum", bufs=4))
+        work_psum = ctx.enter_context(tc.psum_pool(name="work_psum", bufs=4))
+        ctx.enter_context(tc.manual_schedule())
+
+        gb_raw = const.tile([P, GB_COLS], BF16)
+        nc.vector.memset(gb_raw[:], 0.0)
+        nc.sync.dma_start(out=gb_raw[0:GB_ROWS, :], in_=gamma.rearrange("(c k) -> c k", k=GB_COLS))
+        nc.sync.dma_start(out=gb_raw[GB_ROWS : 2 * GB_ROWS, :], in_=beta.rearrange("(c k) -> c k", k=GB_COLS))
+        gain_bf = [const.tile([P, 1], BF16, name="gain_bf%d" % part) for part in range(2)]
+        nc.scalar.dma_start(out=gain_bf[REAL][:], in_=s_re.partition_broadcast(P))
+        nc.scalar.dma_start(out=gain_bf[IMAG][:], in_=s_im.partition_broadcast(P))
+
+        x_raw = [keep.tile([P, 2, D], BF16, name="x_raw%d" % tok) for tok in range(TOKEN_TILES)]
+
+        def load_x(tok):
+            for stream in range(2):
+                nc.sync.dma_start(
+                    out=x_raw[tok][:, stream, :], in_=x_streams[stream][tok * P : (tok + 1) * P, :]
+                )
+
+        w_raw = {}
+
+        def load_chunk(c):
+            rnd, matrix = divmod(c, 2)
+            raw = w_pool.tile([P, 2, D], BF16)
+            rows = weights[matrix][rnd * N_CHUNK : (rnd + 1) * N_CHUNK, :]
+            nc.sync.dma_start(out=raw[:], in_=rows.rearrange("(r p) k -> p r k", p=P))
+            w_raw[c] = raw
+            if c == X1_AFTER_CHUNK:
+                load_x(1)
+
+        load_x(0)
+        for c in range(W_BUFS):
+            load_chunk(c)
+
+        ident = const.tile([P, P], F32)
+        make_identity(nc, ident[:])
+        minus_half = const.tile([P, 1], F32)
+        nc.gpsimd.memset(minus_half[:], -0.5)
+        gb_f32 = const.tile([P, PACK, P], F32)
+        nc.gpsimd.tensor_copy(out=gb_f32[:], in_=gb_raw[:].rearrange("p (j t) -> p t j", t=PACK))
+        gb_ps = work_psum.tile([P, PACK, P], F32, tag="work")
+        for t in range(PACK):
+            nc.tensor.transpose(gb_ps[:, t, :], gb_f32[:, t, :], ident[:])
+        gb_t = const.tile([P, PACK, 2 * GB_ROWS], F32)
+        nc.scalar.copy(out=gb_t[:], in_=gb_ps[:, :, 0 : 2 * GB_ROWS])
+        gain = [const.tile([P, 1], F32, name="gain%d" % part) for part in range(2)]
+        for part in range(2):
+            nc.gpsimd.tensor_copy(out=gain[part][:], in_=gain_bf[part][:])
+
+        w_codes = [
+            keep.tile([P, PASSES * N_CHUNK], U32, name="w_codes%d" % c, align_bytes=64) for c in range(CHUNKS)
+        ]
+        w_scales = [
+            keep.tile([P, PASSES * N_CHUNK], U8, name="w_scales%d" % c, align_bytes=64) for c in range(CHUNKS)
+        ]
+        w_grouped = {}
+
+        def transpose_chunk(c):
+            words = w_raw[c][:].bitcast(F32)
+            grouped = wg_pool.tile([P, PASSES, N_CHUNK, PACK], BF16, align_bytes=64)
+            grouped_words = grouped[:].bitcast(F32)
+            for g in range(PASSES):
+                bank = wt_psum.tile([P, 2, N_CHUNK], F32)
+                for r in range(2):
+                    for u in range(2):
+                        nc.tensor.transpose(
+                            bank[:, u, r * P : (r + 1) * P],
+                            words[:, r, 2 * P * g + u : 2 * P * (g + 1) : 2],
+                            ident[:],
+                        )
+                nc.scalar.copy(out=grouped_words[:, g, :, :], in_=bank[:].rearrange("p u n -> p n u"))
+            w_grouped[c] = grouped
+            if c + W_BUFS < CHUNKS:
+                load_chunk(c + W_BUFS)
+
+        def quantise_chunk(c):
+            nc.vector.quantize_mx(
+                out=w_codes[c][:].bitcast(FP8X4),
+                scales=w_scales[c][:],
+                in_=w_grouped[c][:].rearrange("p g n t -> p (g n t)"),
+            )
+
+        a_codes = [
+            [keep.tile([P, PASSES * P], U32, name="a_codes%d_%d" % (tok, op), align_bytes=64) for op in range(3)]
+            for tok in range(TOKEN_TILES)
+        ]
+        a_scales = [
+            [keep.tile([P, PASSES * P], U8, name="a_scales%d_%d" % (tok, op), align_bytes=64) for op in range(3)]
+            for tok in range(TOKEN_TILES)
+        ]
+        stats = [keep.tile([P, BN_PARTS, 6], F32, name="stats%d" % tok) for tok in range(TOKEN_TILES)]
+        z_tiles = {}
+        planes = {}
+        x_grouped = {}
+
+        def statistics(tok, parts):
+            for i in parts:
+                stream, j = divmod(i, D // BN_COLS)
+                nc.vector.bn_stats(
+                    out=stats[tok][:, i, :], in_=x_raw[tok][:, stream, BN_COLS * j : BN_COLS * (j + 1)]
+                )
+
+        def centre(tok):
+            mv = small.tile([P, 2], F32)
+            nc.vector.bn_aggr(out=mv[:], in_=stats[tok][:].rearrange("p c s -> p (c s)"))
+            var_eps = small.tile([P, 1], F32)
+            nc.vector.tensor_scalar(out=var_eps[:], in0=mv[:, 1:2], scalar1=EPS, scalar2=None, op0=ALU.add)
+            minus_mean = small.tile([P, 1], F32)
+            nc.vector.tensor_scalar(out=minus_mean[:], in0=mv[:, 0:1], scalar1=-1.0, scalar2=None, op0=ALU.mult)
+            rstd = small.tile([P, 1], F32)
+            nc.gpsimd.tensor_tensor(out=rstd[:], in0=var_eps[:], in1=minus_half[:], op=ALU.pow)
+            for piece in range(PIECES):
+                stream, g = divmod(piece, PASSES)
+                z = z_pool.tile([P, PACK, P], F32)
+                engine = nc.vector if stream == REAL else nc.gpsimd
+                engine.tensor_scalar(
+                    out=z[:],
+                    in0=x_raw[tok][:, stream, K_PASS * g : K_PASS * (g + 1)].rearrange("p (j t) -> p t j", t=PACK),
+                    scalar1=minus_mean[:, 0:1],
+                    scalar2=rstd[:, 0:1],
+                    op0=ALU.add,
+                    op1=ALU.mult,
+                )
+                z_tiles[(tok, piece)] = z
+
+        def quantise_operand(tok, op, grouped):
+            nc.vector.quantize_mx(
+                out=a_codes[tok][op][:].bitcast(FP8X4),
+                scales=a_scales[tok][op][:],
+                in_=grouped[:].rearrange("p g k t -> p (g k t)"),
+            )
+
+        def normalise_piece(tok, piece):
+            stream, g = divmod(piece, PASSES)
+            if g == 0:
+                stream_planes = planes_pool.tile([P, PASSES, PACK, P], BF16)
+                planes[(tok, stream)] = stream_planes
+            z = z_tiles[(tok, piece)]
+            z_t = work_psum.tile([P, PACK, P], F32, tag="work")
+            for t in range(PACK):
+                nc.tensor.transpose(z_t[:, t, :], z[:, t, :], ident[:])
+            for t in range(PACK):
+                col = PASSES * stream + g
+                if tok == 0 and piece % 2 == 1:
+                    nc.scalar.activation(
+                        out=planes[(tok, stream)][:, g, t, :],
+                        in_=z_t[:, t, :],
+                        func=ACT.Identity,
+                        scale=gb_t[:, t, col : col + 1],
+                        bias=gb_t[:, t, GB_ROWS + col : GB_ROWS + col + 1],
+                    )
+                else:
+                    nc.vector.tensor_scalar(
+                        out=planes[(tok, stream)][:, g, t, :],
+                        in0=z_t[:, t, :],
+                        scalar1=gb_t[:, t, col : col + 1],
+                        scalar2=gb_t[:, t, GB_ROWS + col : GB_ROWS + col + 1],
+                        op0=ALU.mult,
+                        op1=ALU.add,
+                    )
+            if g == PASSES - 1:
+                grouped = xg_pool.tile([P, PASSES, P, PACK], BF16, align_bytes=64)
+                nc.vector.tensor_copy(out=grouped[:], in_=planes[(tok, stream)][:].rearrange("p g t k -> p g k t"))
+                x_grouped[(tok, stream)] = grouped
+            if piece == PIECES - 1:
+                quantise_operand(tok, NR, x_grouped[(tok, REAL)])
+                quantise_operand(tok, NI, x_grouped[(tok, IMAG)])
+                negated = xg_pool.tile([P, PASSES, P, PACK], BF16, align_bytes=64, tag="grouped")
+                nc.vector.tensor_scalar(
+                    out=negated[:].rearrange("p g k t -> p (g k t)"),
+                    in0=x_grouped[(tok, IMAG)][:].rearrange("p g k t -> p (g k t)"),
+                    scalar1=-1.0,
+                    scalar2=None,
+                    op0=ALU.mult,
+                )
+                quantise_operand(tok, NEG_NI, negated)
+
+        acc = {}
+
+        def multiply(tok, step):
+            rnd = step // 2
+            part = (IMAG, REAL)[step % 2]
+            half = rnd % 2
+            if half == 0:
+                bank = work_psum.tile([P, ACC_COLS], F32, tag="work")
+                acc[part] = bank
+            cols = acc[part][:, half * N_CHUNK : (half + 1) * N_CHUNK]
+            pairs = ((NR, REAL), (NEG_NI, IMAG)) if part == REAL else ((NR, IMAG), (NI, REAL))
+            for i, (op, matrix) in enumerate(pairs):
+                c = 2 * rnd + matrix
+                for g in range(PASSES):
+                    nc.tensor.matmul_mx(
+                        out=cols,
+                        lhsT=a_codes[tok][op][:, g * P : (g + 1) * P].bitcast(FP8X4),
+                        lhsT_scale=a_scales[tok][op][:, g * P : (g + 1) * P],
+                        rhs=w_codes[c][:, g * N_CHUNK : (g + 1) * N_CHUNK].bitcast(FP8X4),
+                        rhs_scale=w_scales[c][:, g * N_CHUNK : (g + 1) * N_CHUNK],
+                        start=(i == 0 and g == 0),
+                        stop=(i == 1 and g == PASSES - 1),
+                    )
+            if half == 1:
+                y = y_pool.tile([P, ACC_COLS], F32)
+                nc.scalar.activation(out=y[:], in_=acc[part][:], func=ACT.Copy, scale=gain[part][:, 0:1])
+                first_col = (rnd // 2) * ACC_COLS
+                nc.sync.dma_start(out=outs[part][tok * P : (tok + 1) * P, first_col : first_col + ACC_COLS], in_=y[:])
+
+        statistics(0, range(BN_PARTS))
+        centre(0)
+        transpose_chunk(0)
+        transpose_chunk(1)
+        quantise_chunk(0)
+        for piece in range(PASSES):
+            normalise_piece(0, piece)
+        transpose_chunk(2)
+        quantise_chunk(1)
+        for piece in range(PASSES, PIECES):
+            normalise_piece(0, piece)
+        transpose_chunk(3)
+        quantise_chunk(2)
+
+        for step in range(STEPS):
+            if T_LEAD + step < CHUNKS:
+                transpose_chunk(T_LEAD + step)
+            if Q_LEAD + step < CHUNKS:
+                quantise_chunk(Q_LEAD + step)
+            if step < STATS_STEPS:
+                share = BN_PARTS // STATS_STEPS
+                statistics(1, range(share * step, share * (step + 1)))
+            if step == STATS_STEPS - 1:
+                centre(1)
+            if PIECE_STEP <= step < PIECE_STEP + PIECES:
+                normalise_piece(1, step - PIECE_STEP)
+            multiply(0, step)
+
+        for step in range(STEPS):
+            multiply(1, step)

@@ -29,7 +29,6 @@ N_CHUNK = 256
 ROUNDS = N_OUT // N_CHUNK
 CHUNKS = 2 * ROUNDS
 STEPS = 2 * ROUNDS
-ACC_COLS = 2 * N_CHUNK
 BN_COLS = 512
 BN_PARTS = 2 * D // BN_COLS
 GB_COLS = K_PASS
@@ -38,9 +37,8 @@ GB_ROWS = 2 * D // GB_COLS
 W_BUFS = 5
 T_LEAD = 4
 Q_LEAD = T_LEAD - 1
-X1_AFTER_CHUNK = 5
-STATS_STEPS = 4
-PIECE_STEP = STATS_STEPS + 1
+FIRST_PARTED = 10
+M1_LAG = 10
 
 FLOPS = 4 * 2 * TOKENS * D * N_OUT
 
@@ -57,14 +55,16 @@ def tile_realimagfourvallinear_pa_kernel(
         const = ctx.enter_context(tc.tile_pool(name="const", bufs=1))
         keep = ctx.enter_context(tc.tile_pool(name="keep", bufs=1))
         small = ctx.enter_context(tc.tile_pool(name="small", bufs=2))
+        x_pool = ctx.enter_context(tc.tile_pool(name="x_pool", bufs=1))
         w_pool = ctx.enter_context(tc.tile_pool(name="w_pool", bufs=W_BUFS))
-        wg_pool = ctx.enter_context(tc.tile_pool(name="wg_pool", bufs=3))
-        z_pool = ctx.enter_context(tc.tile_pool(name="z_pool", bufs=PIECES))
+        part_pool = ctx.enter_context(tc.tile_pool(name="part_pool", bufs=4))
+        wg_pool = ctx.enter_context(tc.tile_pool(name="wg_pool", bufs=5))
+        z_pool = ctx.enter_context(tc.tile_pool(name="z_pool", bufs=8))
         planes_pool = ctx.enter_context(tc.tile_pool(name="planes_pool", bufs=2))
         xg_pool = ctx.enter_context(tc.tile_pool(name="xg_pool", bufs=3))
-        y_pool = ctx.enter_context(tc.tile_pool(name="y_pool", bufs=4))
-        wt_psum = ctx.enter_context(tc.psum_pool(name="wt_psum", bufs=4))
-        work_psum = ctx.enter_context(tc.psum_pool(name="work_psum", bufs=4))
+        y_pool = ctx.enter_context(tc.tile_pool(name="y_pool", bufs=6))
+        turn_psum = ctx.enter_context(tc.psum_pool(name="turn_psum", bufs=5))
+        acc_psum = ctx.enter_context(tc.psum_pool(name="acc_psum", bufs=3))
         ctx.enter_context(tc.manual_schedule())
 
         gb_raw = const.tile([P, GB_COLS], BF16)
@@ -75,13 +75,13 @@ def tile_realimagfourvallinear_pa_kernel(
         nc.scalar.dma_start(out=gain_bf[REAL][:], in_=s_re.partition_broadcast(P))
         nc.scalar.dma_start(out=gain_bf[IMAG][:], in_=s_im.partition_broadcast(P))
 
-        x_raw = [keep.tile([P, 2, D], BF16, name="x_raw%d" % tok) for tok in range(TOKEN_TILES)]
+        x_raw = {}
 
         def load_x(tok):
             for stream in range(2):
-                nc.sync.dma_start(
-                    out=x_raw[tok][:, stream, :], in_=x_streams[stream][tok * P : (tok + 1) * P, :]
-                )
+                raw = x_pool.tile([P, D], BF16, name="x_raw%d" % stream)
+                nc.sync.dma_start(out=raw[:], in_=x_streams[stream][tok * P : (tok + 1) * P, :])
+                x_raw[(tok, stream)] = raw
 
         w_raw = {}
 
@@ -91,8 +91,6 @@ def tile_realimagfourvallinear_pa_kernel(
             rows = weights[matrix][rnd * N_CHUNK : (rnd + 1) * N_CHUNK, :]
             nc.sync.dma_start(out=raw[:], in_=rows.rearrange("(r p) k -> p r k", p=P))
             w_raw[c] = raw
-            if c == X1_AFTER_CHUNK:
-                load_x(1)
 
         load_x(0)
         for c in range(W_BUFS):
@@ -104,7 +102,7 @@ def tile_realimagfourvallinear_pa_kernel(
         nc.gpsimd.memset(minus_half[:], -0.5)
         gb_f32 = const.tile([P, PACK, P], F32)
         nc.gpsimd.tensor_copy(out=gb_f32[:], in_=gb_raw[:].rearrange("p (j t) -> p t j", t=PACK))
-        gb_ps = work_psum.tile([P, PACK, P], F32, tag="work")
+        gb_ps = turn_psum.tile([P, PACK, P], F32, tag="turn")
         for t in range(PACK):
             nc.tensor.transpose(gb_ps[:, t, :], gb_f32[:, t, :], ident[:])
         gb_t = const.tile([P, PACK, 2 * GB_ROWS], F32)
@@ -120,31 +118,53 @@ def tile_realimagfourvallinear_pa_kernel(
             keep.tile([P, PASSES * N_CHUNK], U8, name="w_scales%d" % c, align_bytes=64) for c in range(CHUNKS)
         ]
         w_grouped = {}
+        w_parted = {}
 
-        def transpose_chunk(c):
-            words = w_raw[c][:].bitcast(F32)
-            grouped = wg_pool.tile([P, PASSES, N_CHUNK, PACK], BF16, align_bytes=64)
-            grouped_words = grouped[:].bitcast(F32)
-            for g in range(PASSES):
-                bank = wt_psum.tile([P, 2, N_CHUNK], F32)
-                for r in range(2):
-                    for u in range(2):
-                        nc.tensor.transpose(
-                            bank[:, u, r * P : (r + 1) * P],
-                            words[:, r, 2 * P * g + u : 2 * P * (g + 1) : 2],
-                            ident[:],
-                        )
-                nc.scalar.copy(out=grouped_words[:, g, :, :], in_=bank[:].rearrange("p u n -> p n u"))
-            w_grouped[c] = grouped
+        def load_next(c):
             if c + W_BUFS < CHUNKS:
                 load_chunk(c + W_BUFS)
 
+        def part_chunk(c):
+            if c < FIRST_PARTED or c >= CHUNKS:
+                return
+            for r in range(2):
+                parted = part_pool.tile([P, PASSES, 2, P], F32)
+                copy = nc.scalar.copy if False else nc.vector.tensor_copy
+                copy(
+                    out=parted[:],
+                    in_=w_raw[c][:].bitcast(F32)[:, r, :].rearrange("p (g j u) -> p g u j", g=PASSES, u=2),
+                )
+                w_parted[(c, r)] = parted
+
+        def transpose_chunk(c):
+            if c >= CHUNKS:
+                return
+            words = w_raw[c][:].bitcast(F32)
+            for g in range(PASSES):
+                if g % 2 == 0:
+                    grouped = wg_pool.tile([P, 2, N_CHUNK, PACK], BF16, align_bytes=64)
+                    w_grouped[(c, g // 2)] = grouped
+                bank = turn_psum.tile([P, 2, N_CHUNK], F32, tag="turn")
+                for r in range(2):
+                    for u in range(2):
+                        if c < FIRST_PARTED:
+                            rows = words[:, r, 2 * P * g + u : 2 * P * (g + 1) : 2]
+                        else:
+                            rows = w_parted[(c, r)][:, g, u, :]
+                        nc.tensor.transpose(bank[:, u, r * P : (r + 1) * P], rows, ident[:])
+                nc.scalar.copy(out=grouped[:, g % 2, :, :].bitcast(F32), in_=bank[:].rearrange("p u n -> p n u"))
+            load_next(c)
+
         def quantise_chunk(c):
-            nc.vector.quantize_mx(
-                out=w_codes[c][:].bitcast(FP8X4),
-                scales=w_scales[c][:],
-                in_=w_grouped[c][:].rearrange("p g n t -> p (g n t)"),
-            )
+            if c >= CHUNKS:
+                return
+            for half in range(2):
+                cols = slice(half * 2 * N_CHUNK, (half + 1) * 2 * N_CHUNK)
+                nc.vector.quantize_mx(
+                    out=w_codes[c][:, cols].bitcast(FP8X4),
+                    scales=w_scales[c][:, cols],
+                    in_=w_grouped[(c, half)][:].rearrange("p g n t -> p (g n t)"),
+                )
 
         a_codes = [
             [keep.tile([P, PASSES * P], U32, name="a_codes%d_%d" % (tok, op), align_bytes=64) for op in range(3)]
@@ -155,7 +175,9 @@ def tile_realimagfourvallinear_pa_kernel(
             for tok in range(TOKEN_TILES)
         ]
         stats = [keep.tile([P, BN_PARTS, 6], F32, name="stats%d" % tok) for tok in range(TOKEN_TILES)]
+        scalars = {}
         z_tiles = {}
+        z_turned = {}
         planes = {}
         x_grouped = {}
 
@@ -163,10 +185,10 @@ def tile_realimagfourvallinear_pa_kernel(
             for i in parts:
                 stream, j = divmod(i, D // BN_COLS)
                 nc.vector.bn_stats(
-                    out=stats[tok][:, i, :], in_=x_raw[tok][:, stream, BN_COLS * j : BN_COLS * (j + 1)]
+                    out=stats[tok][:, i, :], in_=x_raw[(tok, stream)][:, BN_COLS * j : BN_COLS * (j + 1)]
                 )
 
-        def centre(tok):
+        def mean_and_rstd(tok):
             mv = small.tile([P, 2], F32)
             nc.vector.bn_aggr(out=mv[:], in_=stats[tok][:].rearrange("p c s -> p (c s)"))
             var_eps = small.tile([P, 1], F32)
@@ -175,19 +197,21 @@ def tile_realimagfourvallinear_pa_kernel(
             nc.vector.tensor_scalar(out=minus_mean[:], in0=mv[:, 0:1], scalar1=-1.0, scalar2=None, op0=ALU.mult)
             rstd = small.tile([P, 1], F32)
             nc.gpsimd.tensor_tensor(out=rstd[:], in0=var_eps[:], in1=minus_half[:], op=ALU.pow)
-            for piece in range(PIECES):
-                stream, g = divmod(piece, PASSES)
-                z = z_pool.tile([P, PACK, P], F32)
-                engine = nc.vector if stream == REAL else nc.gpsimd
-                engine.tensor_scalar(
-                    out=z[:],
-                    in0=x_raw[tok][:, stream, K_PASS * g : K_PASS * (g + 1)].rearrange("p (j t) -> p t j", t=PACK),
-                    scalar1=minus_mean[:, 0:1],
-                    scalar2=rstd[:, 0:1],
-                    op0=ALU.add,
-                    op1=ALU.mult,
-                )
-                z_tiles[(tok, piece)] = z
+            scalars[tok] = (minus_mean, rstd)
+
+        def centre(tok, piece, engine):
+            minus_mean, rstd = scalars[tok]
+            stream, g = divmod(piece, PASSES)
+            z = z_pool.tile([P, PACK, P], F32)
+            engine.tensor_scalar(
+                out=z[:],
+                in0=x_raw[(tok, stream)][:, K_PASS * g : K_PASS * (g + 1)].rearrange("p (j t) -> p t j", t=PACK),
+                scalar1=minus_mean[:, 0:1],
+                scalar2=rstd[:, 0:1],
+                op0=ALU.add,
+                op1=ALU.mult,
+            )
+            z_tiles[(tok, piece)] = z
 
         def quantise_operand(tok, op, grouped):
             nc.vector.quantize_mx(
@@ -196,18 +220,22 @@ def tile_realimagfourvallinear_pa_kernel(
                 in_=grouped[:].rearrange("p g k t -> p (g k t)"),
             )
 
-        def normalise_piece(tok, piece):
+        def turn_piece(tok, piece):
+            z = z_tiles[(tok, piece)]
+            z_t = turn_psum.tile([P, PACK, P], F32, tag="turn")
+            for t in range(PACK):
+                nc.tensor.transpose(z_t[:, t, :], z[:, t, :], ident[:])
+            z_turned[(tok, piece)] = z_t
+
+        def scale_piece(tok, piece, on_scalar):
             stream, g = divmod(piece, PASSES)
             if g == 0:
                 stream_planes = planes_pool.tile([P, PASSES, PACK, P], BF16)
                 planes[(tok, stream)] = stream_planes
-            z = z_tiles[(tok, piece)]
-            z_t = work_psum.tile([P, PACK, P], F32, tag="work")
-            for t in range(PACK):
-                nc.tensor.transpose(z_t[:, t, :], z[:, t, :], ident[:])
+            z_t = z_turned[(tok, piece)]
             for t in range(PACK):
                 col = PASSES * stream + g
-                if tok == 0 and piece % 2 == 1:
+                if on_scalar:
                     nc.scalar.activation(
                         out=planes[(tok, stream)][:, g, t, :],
                         in_=z_t[:, t, :],
@@ -224,33 +252,32 @@ def tile_realimagfourvallinear_pa_kernel(
                         op0=ALU.mult,
                         op1=ALU.add,
                     )
-            if g == PASSES - 1:
-                grouped = xg_pool.tile([P, PASSES, P, PACK], BF16, align_bytes=64)
-                nc.vector.tensor_copy(out=grouped[:], in_=planes[(tok, stream)][:].rearrange("p g t k -> p g k t"))
-                x_grouped[(tok, stream)] = grouped
-            if piece == PIECES - 1:
-                quantise_operand(tok, NR, x_grouped[(tok, REAL)])
-                quantise_operand(tok, NI, x_grouped[(tok, IMAG)])
-                negated = xg_pool.tile([P, PASSES, P, PACK], BF16, align_bytes=64, tag="grouped")
-                nc.vector.tensor_scalar(
-                    out=negated[:].rearrange("p g k t -> p (g k t)"),
-                    in0=x_grouped[(tok, IMAG)][:].rearrange("p g k t -> p (g k t)"),
-                    scalar1=-1.0,
-                    scalar2=None,
-                    op0=ALU.mult,
-                )
-                quantise_operand(tok, NEG_NI, negated)
+
+        def group_stream(tok, stream):
+            grouped = xg_pool.tile([P, PASSES, P, PACK], BF16, align_bytes=64)
+            nc.vector.tensor_copy(out=grouped[:], in_=planes[(tok, stream)][:].rearrange("p g t k -> p g k t"))
+            x_grouped[(tok, stream)] = grouped
+
+        def negate(tok):
+            negated = xg_pool.tile([P, PASSES, P, PACK], BF16, align_bytes=64, tag="grouped")
+            nc.vector.tensor_scalar(
+                out=negated[:].rearrange("p g k t -> p (g k t)"),
+                in0=x_grouped[(tok, IMAG)][:].rearrange("p g k t -> p (g k t)"),
+                scalar1=-1.0,
+                scalar2=None,
+                op0=ALU.mult,
+            )
+            x_grouped[(tok, NEG_NI)] = negated
 
         acc = {}
 
         def multiply(tok, step):
             rnd = step // 2
             part = (IMAG, REAL)[step % 2]
-            half = rnd % 2
-            if half == 0:
-                bank = work_psum.tile([P, ACC_COLS], F32, tag="work")
-                acc[part] = bank
-            cols = acc[part][:, half * N_CHUNK : (half + 1) * N_CHUNK]
+            if step % 2 == 0:
+                bank = acc_psum.tile([P, 2, N_CHUNK], F32, tag="acc")
+                acc[(tok, rnd)] = bank
+            cols = acc[(tok, rnd)][:, step % 2, :]
             pairs = ((NR, REAL), (NEG_NI, IMAG)) if part == REAL else ((NR, IMAG), (NI, REAL))
             for i, (op, matrix) in enumerate(pairs):
                 c = 2 * rnd + matrix
@@ -264,39 +291,81 @@ def tile_realimagfourvallinear_pa_kernel(
                         start=(i == 0 and g == 0),
                         stop=(i == 1 and g == PASSES - 1),
                     )
-            if half == 1:
-                y = y_pool.tile([P, ACC_COLS], F32)
-                nc.scalar.activation(out=y[:], in_=acc[part][:], func=ACT.Copy, scale=gain[part][:, 0:1])
-                first_col = (rnd // 2) * ACC_COLS
-                nc.sync.dma_start(out=outs[part][tok * P : (tok + 1) * P, first_col : first_col + ACC_COLS], in_=y[:])
+
+        def store(tok, step):
+            if step % 2 == 0:
+                return
+            rnd = step // 2
+            for part in (IMAG, REAL):
+                y = y_pool.tile([P, N_CHUNK], F32)
+                nc.scalar.activation(
+                    out=y[:], in_=acc[(tok, rnd)][:, IMAG - part, :], func=ACT.Copy, scale=gain[part][:, 0:1]
+                )
+                nc.sync.dma_start(
+                    out=outs[part][tok * P : (tok + 1) * P, rnd * N_CHUNK : (rnd + 1) * N_CHUNK], in_=y[:]
+                )
 
         statistics(0, range(BN_PARTS))
-        centre(0)
+        mean_and_rstd(0)
+        for piece in range(PASSES):
+            centre(0, piece, nc.vector)
+            centre(0, PASSES + piece, nc.gpsimd)
+        load_x(1)
         transpose_chunk(0)
         transpose_chunk(1)
         quantise_chunk(0)
         for piece in range(PASSES):
-            normalise_piece(0, piece)
+            turn_piece(0, piece)
+            scale_piece(0, piece, piece % 2 == 1)
+        group_stream(0, REAL)
         transpose_chunk(2)
         quantise_chunk(1)
         for piece in range(PASSES, PIECES):
-            normalise_piece(0, piece)
+            turn_piece(0, piece)
+            scale_piece(0, piece, piece % 2 == 1)
+        quantise_operand(0, NR, x_grouped[(0, REAL)])
+        group_stream(0, IMAG)
         transpose_chunk(3)
         quantise_chunk(2)
+        quantise_operand(0, NI, x_grouped[(0, IMAG)])
+        negate(0)
+        quantise_operand(0, NEG_NI, x_grouped[(0, NEG_NI)])
 
-        for step in range(STEPS):
-            if T_LEAD + step < CHUNKS:
-                transpose_chunk(T_LEAD + step)
-            if Q_LEAD + step < CHUNKS:
-                quantise_chunk(Q_LEAD + step)
-            if step < STATS_STEPS:
-                share = BN_PARTS // STATS_STEPS
-                statistics(1, range(share * step, share * (step + 1)))
-            if step == STATS_STEPS - 1:
-                centre(1)
-            if PIECE_STEP <= step < PIECE_STEP + PIECES:
-                normalise_piece(1, step - PIECE_STEP)
-            multiply(0, step)
-
-        for step in range(STEPS):
-            multiply(1, step)
+        for step in range(STEPS + M1_LAG + 1):
+            ln = step - 0
+            if 4 <= ln < 4 + PASSES:
+                for piece in (2 * ln - 8, 2 * ln - 7):
+                    scale_piece(1, piece, piece % 2 == 1)
+            transpose_chunk(T_LEAD + step)
+            quantise_chunk(Q_LEAD + step)
+            part_chunk(T_LEAD + step + 2)
+            if 0 < step <= STEPS:
+                store(0, step - 1)
+            if step > M1_LAG:
+                store(1, step - M1_LAG - 1)
+            if step < STEPS:
+                multiply(0, step)
+            if M1_LAG <= step < STEPS + M1_LAG:
+                multiply(1, step - M1_LAG)
+            if ln == 0:
+                statistics(1, range(4))
+            if ln == 1:
+                statistics(1, range(4, 8))
+                mean_and_rstd(1)
+            if ln == 2:
+                for piece in range(PASSES):
+                    centre(1, piece, nc.vector)
+                    centre(1, PASSES + piece, nc.gpsimd)
+            if 3 <= ln < 3 + PASSES:
+                for piece in (2 * ln - 6, 2 * ln - 5):
+                    turn_piece(1, piece)
+            if ln == 6:
+                group_stream(1, REAL)
+            if ln == 7:
+                quantise_operand(1, NR, x_grouped[(1, REAL)])
+            if ln == 8:
+                group_stream(1, IMAG)
+            if ln == 9:
+                negate(1)
+                quantise_operand(1, NI, x_grouped[(1, IMAG)])
+                quantise_operand(1, NEG_NI, x_grouped[(1, NEG_NI)])

@@ -271,7 +271,7 @@ def tile_realimagfourvallinear_pa_kernel(
 
         acc = {}
 
-        def multiply(tok, step):
+        def multiply(tok, step, between=()):
             rnd = step // 2
             part = (IMAG, REAL)[step % 2]
             if step % 2 == 0:
@@ -281,6 +281,9 @@ def tile_realimagfourvallinear_pa_kernel(
             pairs = ((NR, REAL), (NEG_NI, IMAG)) if part == REAL else ((NR, IMAG), (NI, REAL))
             for i, (op, matrix) in enumerate(pairs):
                 c = 2 * rnd + matrix
+                if i == 1:
+                    for piece in between:
+                        turn_piece(1, piece)
                 for g in range(PASSES):
                     nc.tensor.matmul_mx(
                         out=cols,
@@ -344,7 +347,7 @@ def tile_realimagfourvallinear_pa_kernel(
             if step > M1_LAG:
                 store(1, step - M1_LAG - 1)
             if step < STEPS:
-                multiply(0, step)
+                multiply(0, step, (2 * ln - 6, 2 * ln - 5) if 3 <= ln < 3 + PASSES else ())
             if M1_LAG <= step < STEPS + M1_LAG:
                 multiply(1, step - M1_LAG)
             if ln == 0:
@@ -356,9 +359,6 @@ def tile_realimagfourvallinear_pa_kernel(
                 for piece in range(PASSES):
                     centre(1, piece, nc.vector)
                     centre(1, PASSES + piece, nc.gpsimd)
-            if 3 <= ln < 3 + PASSES:
-                for piece in (2 * ln - 6, 2 * ln - 5):
-                    turn_piece(1, piece)
             if ln == 6:
                 group_stream(1, REAL)
             if ln == 7:

@@ -25,10 +25,14 @@ PACK = 4
 K_PASS = P * PACK
 PASSES = D // K_PASS
 PIECES = 2 * PASSES
-N_CHUNK = 256
-ROUNDS = N_OUT // N_CHUNK
-CHUNKS = 2 * ROUNDS
-STEPS = 2 * ROUNDS
+N_BLOCK = 512
+BLOCKS = N_OUT // N_BLOCK
+C_PASSES = 2
+C_COLS = C_PASSES * K_PASS
+ROW_TILES = N_BLOCK // P
+CHUNKS_A_BLOCK = 2 * PASSES // C_PASSES
+CHUNKS = BLOCKS * CHUNKS_A_BLOCK
+HALVES = 2
 BN_COLS = 512
 BN_PARTS = 2 * D // BN_COLS
 GB_COLS = K_PASS
@@ -38,7 +42,13 @@ W_BUFS = 5
 T_LEAD = 4
 Q_LEAD = T_LEAD - 1
 FIRST_PARTED = 10
-M1_LAG = 10
+STEPS = 4 * BLOCKS
+M1_LAG = 9
+LAST_GROUP = (TOKEN_TILES - 1, 2 * BLOCKS - 1)
+
+WG_BUFS = 5
+Y_BUFS = 4
+V_COPIES = (0, 1, CHUNKS - 3, CHUNKS - 2, CHUNKS - 1)
 
 FLOPS = 4 * 2 * TOKENS * D * N_OUT
 
@@ -58,19 +68,15 @@ def tile_realimagfourvallinear_pa_kernel(
         x_pool = ctx.enter_context(tc.tile_pool(name="x_pool", bufs=1))
         w_pool = ctx.enter_context(tc.tile_pool(name="w_pool", bufs=W_BUFS))
         part_pool = ctx.enter_context(tc.tile_pool(name="part_pool", bufs=4))
-        wg_pool = ctx.enter_context(tc.tile_pool(name="wg_pool", bufs=5))
+        wg_pool = ctx.enter_context(tc.tile_pool(name="wg_pool", bufs=WG_BUFS))
         z_pool = ctx.enter_context(tc.tile_pool(name="z_pool", bufs=8))
         planes_pool = ctx.enter_context(tc.tile_pool(name="planes_pool", bufs=2))
         xg_pool = ctx.enter_context(tc.tile_pool(name="xg_pool", bufs=3))
-        y_pool = ctx.enter_context(tc.tile_pool(name="y_pool", bufs=6))
+        y_pool = ctx.enter_context(tc.tile_pool(name="y_pool", bufs=Y_BUFS))
         turn_psum = ctx.enter_context(tc.psum_pool(name="turn_psum", bufs=5))
         acc_psum = ctx.enter_context(tc.psum_pool(name="acc_psum", bufs=3))
         ctx.enter_context(tc.manual_schedule())
 
-        gb_raw = const.tile([P, GB_COLS], BF16)
-        nc.vector.memset(gb_raw[:], 0.0)
-        nc.sync.dma_start(out=gb_raw[0:GB_ROWS, :], in_=gamma.rearrange("(c k) -> c k", k=GB_COLS))
-        nc.sync.dma_start(out=gb_raw[GB_ROWS : 2 * GB_ROWS, :], in_=beta.rearrange("(c k) -> c k", k=GB_COLS))
         gain_bf = [const.tile([P, 1], BF16, name="gain_bf%d" % part) for part in range(2)]
         nc.scalar.dma_start(out=gain_bf[REAL][:], in_=s_re.partition_broadcast(P))
         nc.scalar.dma_start(out=gain_bf[IMAG][:], in_=s_im.partition_broadcast(P))
@@ -83,16 +89,28 @@ def tile_realimagfourvallinear_pa_kernel(
                 nc.sync.dma_start(out=raw[:], in_=x_streams[stream][tok * P : (tok + 1) * P, :])
                 x_raw[(tok, stream)] = raw
 
+        def place(c):
+            block, j = divmod(c, CHUNKS_A_BLOCK)
+            matrix, first = divmod(j, PASSES // C_PASSES)
+            return block, IMAG - matrix, first * C_PASSES
+
+        def chunk_of(block, matrix, g):
+            return block * CHUNKS_A_BLOCK + (IMAG - matrix) * (PASSES // C_PASSES) + g // C_PASSES, g % C_PASSES
+
         w_raw = {}
 
         def load_chunk(c):
-            rnd, matrix = divmod(c, 2)
-            raw = w_pool.tile([P, 2, D], BF16)
-            rows = weights[matrix][rnd * N_CHUNK : (rnd + 1) * N_CHUNK, :]
+            block, matrix, first = place(c)
+            raw = w_pool.tile([P, ROW_TILES, C_COLS], BF16)
+            rows = weights[matrix][block * N_BLOCK : (block + 1) * N_BLOCK, first * K_PASS : (first + C_PASSES) * K_PASS]
             nc.sync.dma_start(out=raw[:], in_=rows.rearrange("(r p) k -> p r k", p=P))
             w_raw[c] = raw
 
         load_x(0)
+        gb_raw = const.tile([P, GB_COLS], BF16)
+        nc.vector.memset(gb_raw[:], 0.0)
+        nc.sync.dma_start(out=gb_raw[0:GB_ROWS, :], in_=gamma.rearrange("(c k) -> c k", k=GB_COLS))
+        nc.sync.dma_start(out=gb_raw[GB_ROWS : 2 * GB_ROWS, :], in_=beta.rearrange("(c k) -> c k", k=GB_COLS))
         for c in range(W_BUFS):
             load_chunk(c)
 
@@ -112,10 +130,10 @@ def tile_realimagfourvallinear_pa_kernel(
             nc.gpsimd.tensor_copy(out=gain[part][:], in_=gain_bf[part][:])
 
         w_codes = [
-            keep.tile([P, PASSES * N_CHUNK], U32, name="w_codes%d" % c, align_bytes=64) for c in range(CHUNKS)
+            keep.tile([P, C_PASSES * N_BLOCK], U32, name="w_codes%d" % c, align_bytes=64) for c in range(CHUNKS)
         ]
         w_scales = [
-            keep.tile([P, PASSES * N_CHUNK], U8, name="w_scales%d" % c, align_bytes=64) for c in range(CHUNKS)
+            keep.tile([P, C_PASSES * N_BLOCK], U8, name="w_scales%d" % c, align_bytes=64) for c in range(CHUNKS)
         ]
         w_grouped = {}
         w_parted = {}
@@ -127,43 +145,49 @@ def tile_realimagfourvallinear_pa_kernel(
         def part_chunk(c):
             if c < FIRST_PARTED or c >= CHUNKS:
                 return
-            for r in range(2):
-                parted = part_pool.tile([P, PASSES, 2, P], F32)
-                copy = nc.scalar.copy if False else nc.vector.tensor_copy
-                copy(
+            for h in range(C_PASSES):
+                parted = part_pool.tile([P, ROW_TILES, 2, P], F32)
+                nc.vector.tensor_copy(
                     out=parted[:],
-                    in_=w_raw[c][:].bitcast(F32)[:, r, :].rearrange("p (g j u) -> p g u j", g=PASSES, u=2),
+                    in_=w_raw[c][:].bitcast(F32)[:, :, 2 * P * h : 2 * P * (h + 1)].rearrange("p r (j u) -> p r u j", u=2),
                 )
-                w_parted[(c, r)] = parted
+                w_parted[(c, h)] = parted
 
-        def transpose_chunk(c):
+        def transpose_chunk(c, passes=range(C_PASSES)):
             if c >= CHUNKS:
                 return
             words = w_raw[c][:].bitcast(F32)
-            for g in range(PASSES):
-                if g % 2 == 0:
-                    grouped = wg_pool.tile([P, 2, N_CHUNK, PACK], BF16, align_bytes=64)
-                    w_grouped[(c, g // 2)] = grouped
-                bank = turn_psum.tile([P, 2, N_CHUNK], F32, tag="turn")
-                for r in range(2):
-                    for u in range(2):
-                        if c < FIRST_PARTED:
-                            rows = words[:, r, 2 * P * g + u : 2 * P * (g + 1) : 2]
-                        else:
-                            rows = w_parted[(c, r)][:, g, u, :]
-                        nc.tensor.transpose(bank[:, u, r * P : (r + 1) * P], rows, ident[:])
-                nc.scalar.copy(out=grouped[:, g % 2, :, :].bitcast(F32), in_=bank[:].rearrange("p u n -> p n u"))
-            load_next(c)
+            for h in passes:
+                grouped = wg_pool.tile([P, N_BLOCK, PACK], BF16, align_bytes=64)
+                w_grouped[(c, h)] = grouped
+                for b in range(HALVES):
+                    bank = turn_psum.tile([P, 2, 2 * P], F32, tag="turn")
+                    for i in range(2):
+                        r = 2 * b + i
+                        for u in range(2):
+                            if c < FIRST_PARTED:
+                                rows = words[:, r, 2 * P * h + u : 2 * P * (h + 1) : 2]
+                            else:
+                                rows = w_parted[(c, h)][:, r, u, :]
+                            nc.tensor.transpose(bank[:, u, i * P : (i + 1) * P], rows, ident[:])
+                    last = h == C_PASSES - 1 and b == HALVES - 1
+                    copy = nc.vector.tensor_copy if last and c in V_COPIES else nc.scalar.copy
+                    copy(
+                        out=grouped[:, 2 * P * b : 2 * P * (b + 1), :].bitcast(F32),
+                        in_=bank[:].rearrange("p u n -> p n u"),
+                    )
+            if C_PASSES - 1 in passes:
+                load_next(c)
 
         def quantise_chunk(c):
             if c >= CHUNKS:
                 return
-            for half in range(2):
-                cols = slice(half * 2 * N_CHUNK, (half + 1) * 2 * N_CHUNK)
+            for h in range(C_PASSES):
+                cols = slice(h * N_BLOCK, (h + 1) * N_BLOCK)
                 nc.vector.quantize_mx(
                     out=w_codes[c][:, cols].bitcast(FP8X4),
                     scales=w_scales[c][:, cols],
-                    in_=w_grouped[(c, half)][:].rearrange("p g n t -> p (g n t)"),
+                    in_=w_grouped[(c, h)][:].rearrange("p n t -> p (n t)"),
                 )
 
         a_codes = [
@@ -272,41 +296,51 @@ def tile_realimagfourvallinear_pa_kernel(
         acc = {}
 
         def multiply(tok, step, between=()):
-            rnd = step // 2
-            part = (IMAG, REAL)[step % 2]
-            if step % 2 == 0:
-                bank = acc_psum.tile([P, 2, N_CHUNK], F32, tag="acc")
-                acc[(tok, rnd)] = bank
-            cols = acc[(tok, rnd)][:, step % 2, :]
-            pairs = ((NR, REAL), (NEG_NI, IMAG)) if part == REAL else ((NR, IMAG), (NI, REAL))
-            for i, (op, matrix) in enumerate(pairs):
-                c = 2 * rnd + matrix
-                if i == 1:
+            group, half = divmod(step, 2)
+            block, kind = divmod(group, 2)
+            products = (((NR, IMAG), (NI, REAL)), ((NR, REAL), (NEG_NI, IMAG)))[kind]
+            last = (tok, group) == LAST_GROUP
+            if half == 0 or last:
+                bank = acc_psum.tile([P, N_BLOCK], F32, tag="acc")
+                acc[(tok, step) if last else (tok, group)] = bank
+            if last:
+                cols = slice(half * N_BLOCK // 2, (half + 1) * N_BLOCK // 2)
+                work = [(op, matrix, g) for op, matrix in products for g in range(PASSES)]
+            else:
+                cols = slice(0, N_BLOCK)
+                work = [products[half] + (g,) for g in range(PASSES)]
+            bank = acc[(tok, step) if last else (tok, group)]
+            for i, (op, matrix, g) in enumerate(work):
+                if i == len(work) // 2:
                     for piece in between:
                         turn_piece(1, piece)
-                for g in range(PASSES):
-                    nc.tensor.matmul_mx(
-                        out=cols,
-                        lhsT=a_codes[tok][op][:, g * P : (g + 1) * P].bitcast(FP8X4),
-                        lhsT_scale=a_scales[tok][op][:, g * P : (g + 1) * P],
-                        rhs=w_codes[c][:, g * N_CHUNK : (g + 1) * N_CHUNK].bitcast(FP8X4),
-                        rhs_scale=w_scales[c][:, g * N_CHUNK : (g + 1) * N_CHUNK],
-                        start=(i == 0 and g == 0),
-                        stop=(i == 1 and g == PASSES - 1),
-                    )
+                c, h = chunk_of(block, matrix, g)
+                words = slice(h * N_BLOCK + cols.start, h * N_BLOCK + cols.stop)
+                nc.tensor.matmul_mx(
+                    out=bank[:, cols],
+                    lhsT=a_codes[tok][op][:, g * P : (g + 1) * P].bitcast(FP8X4),
+                    lhsT_scale=a_scales[tok][op][:, g * P : (g + 1) * P],
+                    rhs=w_codes[c][:, words].bitcast(FP8X4),
+                    rhs_scale=w_scales[c][:, words],
+                    start=(i == 0 and (half == 0 or last)),
+                    stop=(i == len(work) - 1 and (half == 1 or last)),
+                )
 
         def store(tok, step):
-            if step % 2 == 0:
+            group, half = divmod(step, 2)
+            block, kind = divmod(group, 2)
+            part = (IMAG, REAL)[kind]
+            last = (tok, group) == LAST_GROUP
+            if half == 0 and not last:
                 return
-            rnd = step // 2
-            for part in (IMAG, REAL):
-                y = y_pool.tile([P, N_CHUNK], F32)
-                nc.scalar.activation(
-                    out=y[:], in_=acc[(tok, rnd)][:, IMAG - part, :], func=ACT.Copy, scale=gain[part][:, 0:1]
-                )
-                nc.sync.dma_start(
-                    out=outs[part][tok * P : (tok + 1) * P, rnd * N_CHUNK : (rnd + 1) * N_CHUNK], in_=y[:]
-                )
+            cols = slice(half * N_BLOCK // 2, (half + 1) * N_BLOCK // 2) if last else slice(0, N_BLOCK)
+            bank = acc[(tok, step) if last else (tok, group)]
+            y = y_pool.tile([P, N_BLOCK], F32)
+            nc.scalar.activation(out=y[:, cols], in_=bank[:, cols], func=ACT.Copy, scale=gain[part][:, 0:1])
+            nc.sync.dma_start(
+                out=outs[part][tok * P : (tok + 1) * P, block * N_BLOCK + cols.start : block * N_BLOCK + cols.stop],
+                in_=y[:, cols],
+            )
 
         statistics(0, range(BN_PARTS))
         mean_and_rstd(0)
@@ -335,7 +369,7 @@ def tile_realimagfourvallinear_pa_kernel(
         quantise_operand(0, NEG_NI, x_grouped[(0, NEG_NI)])
 
         for step in range(STEPS + M1_LAG + 1):
-            ln = step - 0
+            ln = step
             if 4 <= ln < 4 + PASSES:
                 for piece in (2 * ln - 8, 2 * ln - 7):
                     scale_piece(1, piece, piece % 2 == 1)

@@ -279,7 +279,11 @@ def tile_realimagfourvallinear_pa_kernel(
 
         def group_stream(tok, stream):
             grouped = xg_pool.tile([P, PASSES, P, PACK], BF16, align_bytes=64)
-            nc.vector.tensor_copy(out=grouped[:], in_=planes[(tok, stream)][:].rearrange("p g t k -> p g k t"))
+            for g in range(PASSES):
+                nc.vector.tensor_copy(
+                    out=grouped[:, g, :, :].rearrange("p (c i) t -> p c t i", i=4),
+                    in_=planes[(tok, stream)][:, g, :, :].rearrange("p t (c i) -> p c t i", i=4),
+                )
             x_grouped[(tok, stream)] = grouped
 
         def negate(tok):

@@ -35,6 +35,9 @@ CHUNKS = BLOCKS * CHUNKS_A_BLOCK
 HALVES = 2
 BN_COLS = 512
 BN_PARTS = 2 * D // BN_COLS
+BN_DIM = 6
+V_PARTS = 6
+STATS_COLS = (BN_DIM * V_PARTS + 3, BN_DIM * BN_PARTS)
 GB_COLS = K_PASS
 GB_ROWS = 2 * D // GB_COLS
 
@@ -46,7 +49,7 @@ STEPS = 4 * BLOCKS
 M1_LAG = 9
 LAST_GROUP = (TOKEN_TILES - 1, 2 * BLOCKS - 1)
 
-WG_BUFS = 5
+WG_BUFS = 3
 Y_BUFS = 4
 V_COPIES = (0, 1, CHUNKS - 3, CHUNKS - 2, CHUNKS - 1)
 
@@ -67,7 +70,7 @@ def tile_realimagfourvallinear_pa_kernel(
         small = ctx.enter_context(tc.tile_pool(name="small", bufs=2))
         x_pool = ctx.enter_context(tc.tile_pool(name="x_pool", bufs=1))
         w_pool = ctx.enter_context(tc.tile_pool(name="w_pool", bufs=W_BUFS))
-        part_pool = ctx.enter_context(tc.tile_pool(name="part_pool", bufs=4))
+        part_pool = ctx.enter_context(tc.tile_pool(name="part_pool", bufs=2))
         wg_pool = ctx.enter_context(tc.tile_pool(name="wg_pool", bufs=WG_BUFS))
         z_pool = ctx.enter_context(tc.tile_pool(name="z_pool", bufs=8))
         planes_pool = ctx.enter_context(tc.tile_pool(name="planes_pool", bufs=2))
@@ -120,11 +123,14 @@ def tile_realimagfourvallinear_pa_kernel(
         nc.gpsimd.memset(minus_half[:], -0.5)
         gb_f32 = const.tile([P, PACK, P], F32)
         nc.gpsimd.tensor_copy(out=gb_f32[:], in_=gb_raw[:].rearrange("p (j t) -> p t j", t=PACK))
-        gb_ps = turn_psum.tile([P, PACK, P], F32, tag="turn")
-        for t in range(PACK):
-            nc.tensor.transpose(gb_ps[:, t, :], gb_f32[:, t, :], ident[:])
         gb_t = const.tile([P, PACK, 2 * GB_ROWS], F32)
-        nc.scalar.copy(out=gb_t[:], in_=gb_ps[:, :, 0 : 2 * GB_ROWS])
+
+        def turn_gamma_and_beta():
+            gb_ps = turn_psum.tile([P, PACK, P], F32, tag="turn")
+            for t in range(PACK):
+                nc.tensor.transpose(gb_ps[:, t, :], gb_f32[:, t, :], ident[:])
+            nc.scalar.copy(out=gb_t[:], in_=gb_ps[:, :, 0 : 2 * GB_ROWS])
+
         gain = [const.tile([P, 1], F32, name="gain%d" % part) for part in range(2)]
         for part in range(2):
             nc.gpsimd.tensor_copy(out=gain[part][:], in_=gain_bf[part][:])
@@ -145,21 +151,20 @@ def tile_realimagfourvallinear_pa_kernel(
         def part_chunk(c):
             if c < FIRST_PARTED or c >= CHUNKS:
                 return
-            for h in range(C_PASSES):
-                parted = part_pool.tile([P, ROW_TILES, 2, P], F32)
-                nc.vector.tensor_copy(
-                    out=parted[:],
-                    in_=w_raw[c][:].bitcast(F32)[:, :, 2 * P * h : 2 * P * (h + 1)].rearrange("p r (j u) -> p r u j", u=2),
-                )
-                w_parted[(c, h)] = parted
+            parted = part_pool.tile([P, ROW_TILES, C_PASSES, 2, P], F32)
+            nc.vector.tensor_copy(
+                out=parted[:].rearrange("p r h u j -> p (r h) u j"),
+                in_=w_raw[c][:].bitcast(F32).rearrange("p r (h j u) -> p (r h) u j", h=C_PASSES, u=2),
+            )
+            w_parted[c] = parted
 
-        def transpose_chunk(c, passes=range(C_PASSES)):
+        def transpose_chunk(c):
             if c >= CHUNKS:
                 return
             words = w_raw[c][:].bitcast(F32)
-            for h in passes:
-                grouped = wg_pool.tile([P, N_BLOCK, PACK], BF16, align_bytes=64)
-                w_grouped[(c, h)] = grouped
+            grouped = wg_pool.tile([P, C_PASSES, N_BLOCK, PACK], BF16, align_bytes=64)
+            w_grouped[c] = grouped
+            for h in range(C_PASSES):
                 for b in range(HALVES):
                     bank = turn_psum.tile([P, 2, 2 * P], F32, tag="turn")
                     for i in range(2):
@@ -168,27 +173,24 @@ def tile_realimagfourvallinear_pa_kernel(
                             if c < FIRST_PARTED:
                                 rows = words[:, r, 2 * P * h + u : 2 * P * (h + 1) : 2]
                             else:
-                                rows = w_parted[(c, h)][:, r, u, :]
+                                rows = w_parted[c][:, r, h, u, :]
                             nc.tensor.transpose(bank[:, u, i * P : (i + 1) * P], rows, ident[:])
                     last = h == C_PASSES - 1 and b == HALVES - 1
                     copy = nc.vector.tensor_copy if last and c in V_COPIES else nc.scalar.copy
                     copy(
-                        out=grouped[:, 2 * P * b : 2 * P * (b + 1), :].bitcast(F32),
+                        out=grouped[:, h, 2 * P * b : 2 * P * (b + 1), :].bitcast(F32),
                         in_=bank[:].rearrange("p u n -> p n u"),
                     )
-            if C_PASSES - 1 in passes:
-                load_next(c)
+            load_next(c)
 
         def quantise_chunk(c):
             if c >= CHUNKS:
                 return
-            for h in range(C_PASSES):
-                cols = slice(h * N_BLOCK, (h + 1) * N_BLOCK)
-                nc.vector.quantize_mx(
-                    out=w_codes[c][:, cols].bitcast(FP8X4),
-                    scales=w_scales[c][:, cols],
-                    in_=w_grouped[(c, h)][:].rearrange("p n t -> p (n t)"),
-                )
+            nc.vector.quantize_mx(
+                out=w_codes[c][:].bitcast(FP8X4),
+                scales=w_scales[c][:],
+                in_=w_grouped[c][:].rearrange("p h n t -> p (h n t)"),
+            )
 
         a_codes = [
             [keep.tile([P, PASSES * P], U32, name="a_codes%d_%d" % (tok, op), align_bytes=64) for op in range(3)]
@@ -198,7 +200,7 @@ def tile_realimagfourvallinear_pa_kernel(
             [keep.tile([P, PASSES * P], U8, name="a_scales%d_%d" % (tok, op), align_bytes=64) for op in range(3)]
             for tok in range(TOKEN_TILES)
         ]
-        stats = [keep.tile([P, BN_PARTS, 6], F32, name="stats%d" % tok) for tok in range(TOKEN_TILES)]
+        stats = [keep.tile([P, STATS_COLS[tok]], F32, name="stats%d" % tok) for tok in range(TOKEN_TILES)]
         scalars = {}
         z_tiles = {}
         z_turned = {}
@@ -209,12 +211,23 @@ def tile_realimagfourvallinear_pa_kernel(
             for i in parts:
                 stream, j = divmod(i, D // BN_COLS)
                 nc.vector.bn_stats(
-                    out=stats[tok][:, i, :], in_=x_raw[(tok, stream)][:, BN_COLS * j : BN_COLS * (j + 1)]
+                    out=stats[tok][:, BN_DIM * i : BN_DIM * (i + 1)], in_=x_raw[(tok, stream)][:, BN_COLS * j : BN_COLS * (j + 1)]
                 )
+
+        def statistics_on_scalar(tok, first):
+            cols = x_raw[(tok, IMAG)][:, BN_COLS * first - D : D]
+            n = 2 * D - BN_COLS * first
+            count, mean, spread = [stats[tok][:, BN_DIM * first + i : BN_DIM * first + i + 1] for i in range(3)]
+            nc.vector.memset(count, float(n))
+            unused = const.tile([P, n], BF16)
+            minus = const.tile([P, 1], F32)
+            nc.scalar.activation(out=unused[:], in_=cols, func=ACT.Copy, scale=1.0 / n, accum_out=mean)
+            nc.scalar.activation(out=minus[:], in_=mean, func=ACT.Copy, scale=-1.0)
+            nc.scalar.activation(out=unused[:], in_=cols, func=ACT.Square, bias=minus[:, 0:1], accum_out=spread)
 
         def mean_and_rstd(tok):
             mv = small.tile([P, 2], F32)
-            nc.vector.bn_aggr(out=mv[:], in_=stats[tok][:].rearrange("p c s -> p (c s)"))
+            nc.vector.bn_aggr(out=mv[:], in_=stats[tok][:])
             var_eps = small.tile([P, 1], F32)
             nc.vector.tensor_scalar(out=var_eps[:], in0=mv[:, 1:2], scalar1=EPS, scalar2=None, op0=ALU.add)
             minus_mean = small.tile([P, 1], F32)
@@ -254,14 +267,14 @@ def tile_realimagfourvallinear_pa_kernel(
         def scale_piece(tok, piece, on_scalar):
             stream, g = divmod(piece, PASSES)
             if g == 0:
-                stream_planes = planes_pool.tile([P, PASSES, PACK, P], BF16)
+                stream_planes = planes_pool.tile([P, PACK, PASSES, P], BF16)
                 planes[(tok, stream)] = stream_planes
             z_t = z_turned[(tok, piece)]
             for t in range(PACK):
                 col = PASSES * stream + g
                 if on_scalar:
                     nc.scalar.activation(
-                        out=planes[(tok, stream)][:, g, t, :],
+                        out=planes[(tok, stream)][:, t, g, :],
                         in_=z_t[:, t, :],
                         func=ACT.Identity,
                         scale=gb_t[:, t, col : col + 1],
@@ -269,7 +282,7 @@ def tile_realimagfourvallinear_pa_kernel(
                     )
                 else:
                     nc.vector.tensor_scalar(
-                        out=planes[(tok, stream)][:, g, t, :],
+                        out=planes[(tok, stream)][:, t, g, :],
                         in0=z_t[:, t, :],
                         scalar1=gb_t[:, t, col : col + 1],
                         scalar2=gb_t[:, t, GB_ROWS + col : GB_ROWS + col + 1],
@@ -279,11 +292,10 @@ def tile_realimagfourvallinear_pa_kernel(
 
         def group_stream(tok, stream):
             grouped = xg_pool.tile([P, PASSES, P, PACK], BF16, align_bytes=64)
-            for g in range(PASSES):
-                nc.vector.tensor_copy(
-                    out=grouped[:, g, :, :].rearrange("p (c i) t -> p c t i", i=4),
-                    in_=planes[(tok, stream)][:, g, :, :].rearrange("p t (c i) -> p c t i", i=4),
-                )
+            nc.vector.tensor_copy(
+                out=grouped[:].rearrange("p g k t -> p (g k) t").rearrange("p (c i) t -> p c t i", i=4),
+                in_=planes[(tok, stream)][:].rearrange("p t g k -> p t (g k)").rearrange("p t (c i) -> p c t i", i=4),
+            )
             x_grouped[(tok, stream)] = grouped
 
         def negate(tok):
@@ -346,7 +358,9 @@ def tile_realimagfourvallinear_pa_kernel(
                 in_=y[:, cols],
             )
 
-        statistics(0, range(BN_PARTS))
+        statistics_on_scalar(0, V_PARTS)
+        statistics(0, range(V_PARTS))
+        turn_gamma_and_beta()
         mean_and_rstd(0)
         for piece in range(PASSES):
             centre(0, piece, nc.vector)

@@ -36,8 +36,8 @@ HALVES = 2
 BN_COLS = 512
 BN_PARTS = 2 * D // BN_COLS
 BN_DIM = 6
-V_PARTS = 6
-STATS_COLS = (BN_DIM * V_PARTS + 3, BN_DIM * BN_PARTS)
+V_PARTS = (0, 1, 4, 5, 6, 7)
+STATS_COLS = (BN_DIM * len(V_PARTS) + 3, BN_DIM * BN_PARTS)
 GB_COLS = K_PASS
 GB_ROWS = 2 * D // GB_COLS
 
@@ -51,7 +51,10 @@ LAST_GROUP = (TOKEN_TILES - 1, 2 * BLOCKS - 1)
 
 WG_BUFS = 3
 Y_BUFS = 4
-V_COPIES = (0, 1, CHUNKS - 3, CHUNKS - 2, CHUNKS - 1)
+V_COPIES = (CHUNKS - 2, CHUNKS - 1)
+SCALAR_PIECES = ((1, 3, 7), (1, 3, 5, 7))
+TURN_STEPS = {4: (0, 1, 2, 3), 5: (4, 5, 6, 7)}
+TURN_STEPS_AFTER = {5: (0, 1, 2, 3), 6: (4, 5, 6, 7)}
 
 FLOPS = 4 * 2 * TOKENS * D * N_OUT
 
@@ -86,10 +89,12 @@ def tile_realimagfourvallinear_pa_kernel(
 
         x_raw = {}
 
-        def load_x(tok):
+        def load_x(tok, parts=1):
             for stream in range(2):
                 raw = x_pool.tile([P, D], BF16, name="x_raw%d" % stream)
-                nc.sync.dma_start(out=raw[:], in_=x_streams[stream][tok * P : (tok + 1) * P, :])
+                for part in range(parts):
+                    cols = slice(part * D // parts, (part + 1) * D // parts)
+                    nc.sync.dma_start(out=raw[:, cols], in_=x_streams[stream][tok * P : (tok + 1) * P, cols])
                 x_raw[(tok, stream)] = raw
 
         def place(c):
@@ -102,20 +107,23 @@ def tile_realimagfourvallinear_pa_kernel(
 
         w_raw = {}
 
-        def load_chunk(c):
+        def load_chunk(c, parts=1):
             block, matrix, first = place(c)
             raw = w_pool.tile([P, ROW_TILES, C_COLS], BF16)
-            rows = weights[matrix][block * N_BLOCK : (block + 1) * N_BLOCK, first * K_PASS : (first + C_PASSES) * K_PASS]
-            nc.sync.dma_start(out=raw[:], in_=rows.rearrange("(r p) k -> p r k", p=P))
+            n = ROW_TILES // parts
+            for part in range(parts):
+                row = block * N_BLOCK + part * n * P
+                rows = weights[matrix][row : row + n * P, first * K_PASS : (first + C_PASSES) * K_PASS]
+                nc.sync.dma_start(out=raw[:, part * n : (part + 1) * n, :], in_=rows.rearrange("(r p) k -> p r k", p=P))
             w_raw[c] = raw
 
-        load_x(0)
+        load_x(0, 2)
         gb_raw = const.tile([P, GB_COLS], BF16)
         nc.vector.memset(gb_raw[:], 0.0)
         nc.sync.dma_start(out=gb_raw[0:GB_ROWS, :], in_=gamma.rearrange("(c k) -> c k", k=GB_COLS))
         nc.sync.dma_start(out=gb_raw[GB_ROWS : 2 * GB_ROWS, :], in_=beta.rearrange("(c k) -> c k", k=GB_COLS))
         for c in range(W_BUFS):
-            load_chunk(c)
+            load_chunk(c, HALVES if c == 0 else 1)
 
         ident = const.tile([P, P], F32)
         make_identity(nc, ident[:])
@@ -164,8 +172,8 @@ def tile_realimagfourvallinear_pa_kernel(
             words = w_raw[c][:].bitcast(F32)
             grouped = wg_pool.tile([P, C_PASSES, N_BLOCK, PACK], BF16, align_bytes=64)
             w_grouped[c] = grouped
-            for h in range(C_PASSES):
-                for b in range(HALVES):
+            for b in range(HALVES):
+                for h in range(C_PASSES):
                     bank = turn_psum.tile([P, 2, 2 * P], F32, tag="turn")
                     for i in range(2):
                         r = 2 * b + i
@@ -175,8 +183,7 @@ def tile_realimagfourvallinear_pa_kernel(
                             else:
                                 rows = w_parted[c][:, r, h, u, :]
                             nc.tensor.transpose(bank[:, u, i * P : (i + 1) * P], rows, ident[:])
-                    last = h == C_PASSES - 1 and b == HALVES - 1
-                    copy = nc.vector.tensor_copy if last and c in V_COPIES else nc.scalar.copy
+                    copy = nc.vector.tensor_copy if b == HALVES - 1 and c in V_COPIES else nc.scalar.copy
                     copy(
                         out=grouped[:, h, 2 * P * b : 2 * P * (b + 1), :].bitcast(F32),
                         in_=bank[:].rearrange("p u n -> p n u"),
@@ -207,17 +214,18 @@ def tile_realimagfourvallinear_pa_kernel(
         planes = {}
         x_grouped = {}
 
-        def statistics(tok, parts):
-            for i in parts:
+        def statistics(tok, parts, start=0):
+            for n, i in enumerate(parts):
                 stream, j = divmod(i, D // BN_COLS)
+                i = start + n
                 nc.vector.bn_stats(
                     out=stats[tok][:, BN_DIM * i : BN_DIM * (i + 1)], in_=x_raw[(tok, stream)][:, BN_COLS * j : BN_COLS * (j + 1)]
                 )
 
-        def statistics_on_scalar(tok, first):
-            cols = x_raw[(tok, IMAG)][:, BN_COLS * first - D : D]
-            n = 2 * D - BN_COLS * first
-            count, mean, spread = [stats[tok][:, BN_DIM * first + i : BN_DIM * first + i + 1] for i in range(3)]
+        def statistics_on_scalar(tok):
+            n = D // 2
+            cols = x_raw[(tok, REAL)][:, n:D]
+            count, mean, spread = [stats[tok][:, STATS_COLS[tok] - 3 + i : STATS_COLS[tok] - 2 + i] for i in range(3)]
             nc.vector.memset(count, float(n))
             unused = const.tile([P, n], BF16)
             minus = const.tile([P, 1], F32)
@@ -358,66 +366,73 @@ def tile_realimagfourvallinear_pa_kernel(
                 in_=y[:, cols],
             )
 
-        statistics_on_scalar(0, V_PARTS)
-        statistics(0, range(V_PARTS))
+        def turn_and_scale(tok, pieces):
+            for piece in pieces:
+                turn_piece(tok, piece)
+                scale_piece(tok, piece, piece in SCALAR_PIECES[tok])
+
+        def prepare(c):
+            transpose_chunk(c)
+            quantise_chunk(c - 1)
+            part_chunk(c + 2)
+
+        real, imag = range(PASSES), range(PASSES, PIECES)
+        statistics_on_scalar(0)
+        statistics(0, V_PARTS)
         turn_gamma_and_beta()
         mean_and_rstd(0)
-        for piece in range(PASSES):
+        for piece in real:
             centre(0, piece, nc.vector)
-            centre(0, PASSES + piece, nc.gpsimd)
-        load_x(1)
         transpose_chunk(0)
-        transpose_chunk(1)
-        quantise_chunk(0)
-        for piece in range(PASSES):
-            turn_piece(0, piece)
-            scale_piece(0, piece, piece % 2 == 1)
+        turn_and_scale(0, real)
+        for piece in imag:
+            centre(0, piece, nc.gpsimd)
+        load_x(1)
+        prepare(1)
         group_stream(0, REAL)
+        turn_and_scale(0, imag)
         transpose_chunk(2)
-        quantise_chunk(1)
-        for piece in range(PASSES, PIECES):
-            turn_piece(0, piece)
-            scale_piece(0, piece, piece % 2 == 1)
         quantise_operand(0, NR, x_grouped[(0, REAL)])
+        quantise_chunk(1)
         group_stream(0, IMAG)
         transpose_chunk(3)
-        quantise_chunk(2)
         quantise_operand(0, NI, x_grouped[(0, IMAG)])
+        quantise_chunk(2)
         negate(0)
         quantise_operand(0, NEG_NI, x_grouped[(0, NEG_NI)])
+        prepare(4)
 
         for step in range(STEPS + M1_LAG + 1):
-            ln = step
-            if 4 <= ln < 4 + PASSES:
-                for piece in (2 * ln - 8, 2 * ln - 7):
-                    scale_piece(1, piece, piece % 2 == 1)
-            transpose_chunk(T_LEAD + step)
-            quantise_chunk(Q_LEAD + step)
-            part_chunk(T_LEAD + step + 2)
+            if step in TURN_STEPS_AFTER:
+                for piece in TURN_STEPS_AFTER[step]:
+                    scale_piece(1, piece, piece in SCALAR_PIECES[1])
+            if step == 6:
+                group_stream(1, REAL)
+            if step == 7:
+                quantise_operand(1, NR, x_grouped[(1, REAL)])
+                group_stream(1, IMAG)
+            if step == 8:
+                quantise_operand(1, NI, x_grouped[(1, IMAG)])
+                negate(1)
+            if step == 9:
+                quantise_operand(1, NEG_NI, x_grouped[(1, NEG_NI)])
+            if step != 4:
+                prepare(5 + step if step < 4 else 4 + step)
             if 0 < step <= STEPS:
                 store(0, step - 1)
             if step > M1_LAG:
                 store(1, step - M1_LAG - 1)
             if step < STEPS:
-                multiply(0, step, (2 * ln - 6, 2 * ln - 5) if 3 <= ln < 3 + PASSES else ())
+                multiply(0, step, TURN_STEPS.get(step, ()))
             if M1_LAG <= step < STEPS + M1_LAG:
                 multiply(1, step - M1_LAG)
-            if ln == 0:
+            if step == 0:
                 statistics(1, range(4))
-            if ln == 1:
-                statistics(1, range(4, 8))
+            if step == 1:
+                statistics(1, range(4, 8), 4)
                 mean_and_rstd(1)
-            if ln == 2:
-                for piece in range(PASSES):
+            if step == 2:
+                for piece in real:
                     centre(1, piece, nc.vector)
-                    centre(1, PASSES + piece, nc.gpsimd)
-            if ln == 6:
-                group_stream(1, REAL)
-            if ln == 7:
-                quantise_operand(1, NR, x_grouped[(1, REAL)])
-            if ln == 8:
-                group_stream(1, IMAG)
-            if ln == 9:
-                negate(1)
-                quantise_operand(1, NI, x_grouped[(1, IMAG)])
-                quantise_operand(1, NEG_NI, x_grouped[(1, NEG_NI)])
+                for piece in imag:
+                    centre(1, piece, nc.gpsimd)

from contextlib import ExitStack

import concourse.mybir as mybir
from concourse.masks import make_identity

F32 = mybir.dt.float32
BF16 = mybir.dt.bfloat16
U32 = mybir.dt.uint32
U8 = mybir.dt.uint8
FP8X4 = mybir.dt.float8_e4m3fn_x4
ALU = mybir.AluOpType
ACT = mybir.ActivationFunctionType

P = 128
TOKENS = 256
TOKEN_TILES = TOKENS // P
D = 2048
N_OUT = 2048
EPS = 1e-6

REAL, IMAG = 0, 1
NR, NI, NEG_NI = 0, 1, 2

PACK = 4
K_PASS = P * PACK
PASSES = D // K_PASS
PIECES = 2 * PASSES
N_BLOCK = 512
BLOCKS = N_OUT // N_BLOCK
C_PASSES = 2
C_COLS = C_PASSES * K_PASS
ROW_TILES = N_BLOCK // P
CHUNKS_A_BLOCK = 2 * PASSES // C_PASSES
CHUNKS = BLOCKS * CHUNKS_A_BLOCK
HALVES = 2
BN_COLS = 512
BN_PARTS = 2 * D // BN_COLS
BN_DIM = 6
V_PARTS = (0, 1, 4, 5, 6, 7)
STATS_COLS = (BN_DIM * len(V_PARTS) + 3, BN_DIM * BN_PARTS)
GB_COLS = K_PASS
GB_ROWS = 2 * D // GB_COLS

W_BUFS = 5
T_LEAD = 4
Q_LEAD = T_LEAD - 1
FIRST_PARTED = 10
STEPS = 4 * BLOCKS
M1_LAG = 9
LAST_GROUP = (TOKEN_TILES - 1, 2 * BLOCKS - 1)

WG_BUFS = 3
Y_BUFS = 4
V_COPIES = (CHUNKS - 2, CHUNKS - 1)
SCALAR_PIECES = ((1, 3, 7), (1, 3, 5, 7))
TURN_STEPS = {4: (0, 1, 2, 3), 5: (4, 5, 6, 7)}
TURN_STEPS_AFTER = {5: (0, 1, 2, 3), 6: (4, 5, 6, 7)}

FLOPS = 4 * 2 * TOKENS * D * N_OUT


def tile_realimagfourvallinear_pa_kernel(
    tc, x_real, x_imag, qw_re, qw_im, gamma, beta, s_re, s_im, out_0, out_1
):
    nc = tc.nc
    x_streams = (x_real.flatten_outer_dims(), x_imag.flatten_outer_dims())
    weights = (qw_re, qw_im)
    outs = (out_0.flatten_outer_dims(), out_1.flatten_outer_dims())

    with ExitStack() as ctx:
        const = ctx.enter_context(tc.tile_pool(name="const", bufs=1))
        keep = ctx.enter_context(tc.tile_pool(name="keep", bufs=1))
        small = ctx.enter_context(tc.tile_pool(name="small", bufs=2))
        x_pool = ctx.enter_context(tc.tile_pool(name="x_pool", bufs=1))
        w_pool = ctx.enter_context(tc.tile_pool(name="w_pool", bufs=W_BUFS))
        part_pool = ctx.enter_context(tc.tile_pool(name="part_pool", bufs=2))
        wg_pool = ctx.enter_context(tc.tile_pool(name="wg_pool", bufs=WG_BUFS))
        z_pool = ctx.enter_context(tc.tile_pool(name="z_pool", bufs=8))
        planes_pool = ctx.enter_context(tc.tile_pool(name="planes_pool", bufs=2))
        xg_pool = ctx.enter_context(tc.tile_pool(name="xg_pool", bufs=3))
        y_pool = ctx.enter_context(tc.tile_pool(name="y_pool", bufs=Y_BUFS))
        turn_psum = ctx.enter_context(tc.psum_pool(name="turn_psum", bufs=5))
        acc_psum = ctx.enter_context(tc.psum_pool(name="acc_psum", bufs=3))
        ctx.enter_context(tc.manual_schedule())

        gain_bf = [const.tile([P, 1], BF16, name="gain_bf%d" % part) for part in range(2)]
        nc.scalar.dma_start(out=gain_bf[REAL][:], in_=s_re.partition_broadcast(P))
        nc.scalar.dma_start(out=gain_bf[IMAG][:], in_=s_im.partition_broadcast(P))

        x_raw = {}

        def load_x(tok, parts=1):
            for stream in range(2):
                raw = x_pool.tile([P, D], BF16, name="x_raw%d" % stream)
                for part in range(parts):
                    cols = slice(part * D // parts, (part + 1) * D // parts)
                    nc.sync.dma_start(out=raw[:, cols], in_=x_streams[stream][tok * P : (tok + 1) * P, cols])
                x_raw[(tok, stream)] = raw

        def place(c):
            block, j = divmod(c, CHUNKS_A_BLOCK)
            matrix, first = divmod(j, PASSES // C_PASSES)
            return block, IMAG - matrix, first * C_PASSES

        def chunk_of(block, matrix, g):
            return block * CHUNKS_A_BLOCK + (IMAG - matrix) * (PASSES // C_PASSES) + g // C_PASSES, g % C_PASSES

        w_raw = {}

        def load_chunk(c, parts=1):
            block, matrix, first = place(c)
            raw = w_pool.tile([P, ROW_TILES, C_COLS], BF16)
            n = ROW_TILES // parts
            for part in range(parts):
                row = block * N_BLOCK + part * n * P
                rows = weights[matrix][row : row + n * P, first * K_PASS : (first + C_PASSES) * K_PASS]
                nc.sync.dma_start(out=raw[:, part * n : (part + 1) * n, :], in_=rows.rearrange("(r p) k -> p r k", p=P))
            w_raw[c] = raw

        load_x(0, 2)
        gb_raw = const.tile([P, GB_COLS], BF16)
        nc.vector.memset(gb_raw[:], 0.0)
        nc.sync.dma_start(out=gb_raw[0:GB_ROWS, :], in_=gamma.rearrange("(c k) -> c k", k=GB_COLS))
        nc.sync.dma_start(out=gb_raw[GB_ROWS : 2 * GB_ROWS, :], in_=beta.rearrange("(c k) -> c k", k=GB_COLS))
        for c in range(W_BUFS):
            load_chunk(c, HALVES if c == 0 else 1)

        ident = const.tile([P, P], F32)
        make_identity(nc, ident[:])
        minus_half = const.tile([P, 1], F32)
        nc.gpsimd.memset(minus_half[:], -0.5)
        gb_f32 = const.tile([P, PACK, P], F32)
        nc.gpsimd.tensor_copy(out=gb_f32[:], in_=gb_raw[:].rearrange("p (j t) -> p t j", t=PACK))
        gb_t = const.tile([P, PACK, 2 * GB_ROWS], F32)

        def turn_gamma_and_beta():
            gb_ps = turn_psum.tile([P, PACK, P], F32, tag="turn")
            for t in range(PACK):
                nc.tensor.transpose(gb_ps[:, t, :], gb_f32[:, t, :], ident[:])
            nc.scalar.copy(out=gb_t[:], in_=gb_ps[:, :, 0 : 2 * GB_ROWS])

        gain = [const.tile([P, 1], F32, name="gain%d" % part) for part in range(2)]
        for part in range(2):
            nc.gpsimd.tensor_copy(out=gain[part][:], in_=gain_bf[part][:])

        w_codes = [
            keep.tile([P, C_PASSES * N_BLOCK], U32, name="w_codes%d" % c, align_bytes=64) for c in range(CHUNKS)
        ]
        w_scales = [
            keep.tile([P, C_PASSES * N_BLOCK], U8, name="w_scales%d" % c, align_bytes=64) for c in range(CHUNKS)
        ]
        w_grouped = {}
        w_parted = {}

        def load_next(c):
            if c + W_BUFS < CHUNKS:
                load_chunk(c + W_BUFS)

        def part_chunk(c):
            if c < FIRST_PARTED or c >= CHUNKS:
                return
            parted = part_pool.tile([P, ROW_TILES, C_PASSES, 2, P], F32)
            nc.vector.tensor_copy(
                out=parted[:].rearrange("p r h u j -> p (r h) u j"),
                in_=w_raw[c][:].bitcast(F32).rearrange("p r (h j u) -> p (r h) u j", h=C_PASSES, u=2),
            )
            w_parted[c] = parted

        def transpose_chunk(c):
            if c >= CHUNKS:
                return
            words = w_raw[c][:].bitcast(F32)
            grouped = wg_pool.tile([P, C_PASSES, N_BLOCK, PACK], BF16, align_bytes=64)
            w_grouped[c] = grouped
            for b in range(HALVES):
                for h in range(C_PASSES):
                    bank = turn_psum.tile([P, 2, 2 * P], F32, tag="turn")
                    for i in range(2):
                        r = 2 * b + i
                        for u in range(2):
                            if c < FIRST_PARTED:
                                rows = words[:, r, 2 * P * h + u : 2 * P * (h + 1) : 2]
                            else:
                                rows = w_parted[c][:, r, h, u, :]
                            nc.tensor.transpose(bank[:, u, i * P : (i + 1) * P], rows, ident[:])
                    copy = nc.vector.tensor_copy if b == HALVES - 1 and c in V_COPIES else nc.scalar.copy
                    copy(
                        out=grouped[:, h, 2 * P * b : 2 * P * (b + 1), :].bitcast(F32),
                        in_=bank[:].rearrange("p u n -> p n u"),
                    )
            load_next(c)

        def quantise_chunk(c):
            if c >= CHUNKS:
                return
            nc.vector.quantize_mx(
                out=w_codes[c][:].bitcast(FP8X4),
                scales=w_scales[c][:],
                in_=w_grouped[c][:].rearrange("p h n t -> p (h n t)"),
            )

        a_codes = [
            [keep.tile([P, PASSES * P], U32, name="a_codes%d_%d" % (tok, op), align_bytes=64) for op in range(3)]
            for tok in range(TOKEN_TILES)
        ]
        a_scales = [
            [keep.tile([P, PASSES * P], U8, name="a_scales%d_%d" % (tok, op), align_bytes=64) for op in range(3)]
            for tok in range(TOKEN_TILES)
        ]
        stats = [keep.tile([P, STATS_COLS[tok]], F32, name="stats%d" % tok) for tok in range(TOKEN_TILES)]
        scalars = {}
        z_tiles = {}
        z_turned = {}
        planes = {}
        x_grouped = {}

        def statistics(tok, parts, start=0):
            for n, i in enumerate(parts):
                stream, j = divmod(i, D // BN_COLS)
                i = start + n
                nc.vector.bn_stats(
                    out=stats[tok][:, BN_DIM * i : BN_DIM * (i + 1)], in_=x_raw[(tok, stream)][:, BN_COLS * j : BN_COLS * (j + 1)]
                )

        def statistics_on_scalar(tok):
            n = D // 2
            cols = x_raw[(tok, REAL)][:, n:D]
            count, mean, spread = [stats[tok][:, STATS_COLS[tok] - 3 + i : STATS_COLS[tok] - 2 + i] for i in range(3)]
            nc.vector.memset(count, float(n))
            unused = const.tile([P, n], BF16)
            minus = const.tile([P, 1], F32)
            nc.scalar.activation(out=unused[:], in_=cols, func=ACT.Copy, scale=1.0 / n, accum_out=mean)
            nc.scalar.activation(out=minus[:], in_=mean, func=ACT.Copy, scale=-1.0)
            nc.scalar.activation(out=unused[:], in_=cols, func=ACT.Square, bias=minus[:, 0:1], accum_out=spread)

        def mean_and_rstd(tok):
            mv = small.tile([P, 2], F32)
            nc.vector.bn_aggr(out=mv[:], in_=stats[tok][:])
            var_eps = small.tile([P, 1], F32)
            nc.vector.tensor_scalar(out=var_eps[:], in0=mv[:, 1:2], scalar1=EPS, scalar2=None, op0=ALU.add)
            minus_mean = small.tile([P, 1], F32)
            nc.vector.tensor_scalar(out=minus_mean[:], in0=mv[:, 0:1], scalar1=-1.0, scalar2=None, op0=ALU.mult)
            rstd = small.tile([P, 1], F32)
            nc.gpsimd.tensor_tensor(out=rstd[:], in0=var_eps[:], in1=minus_half[:], op=ALU.pow)
            scalars[tok] = (minus_mean, rstd)

        def centre(tok, piece, engine):
            minus_mean, rstd = scalars[tok]
            stream, g = divmod(piece, PASSES)
            z = z_pool.tile([P, PACK, P], F32)
            engine.tensor_scalar(
                out=z[:],
                in0=x_raw[(tok, stream)][:, K_PASS * g : K_PASS * (g + 1)].rearrange("p (j t) -> p t j", t=PACK),
                scalar1=minus_mean[:, 0:1],
                scalar2=rstd[:, 0:1],
                op0=ALU.add,
                op1=ALU.mult,
            )
            z_tiles[(tok, piece)] = z

        def quantise_operand(tok, op, grouped):
            nc.vector.quantize_mx(
                out=a_codes[tok][op][:].bitcast(FP8X4),
                scales=a_scales[tok][op][:],
                in_=grouped[:].rearrange("p g k t -> p (g k t)"),
            )

        def turn_piece(tok, piece):
            z = z_tiles[(tok, piece)]
            z_t = turn_psum.tile([P, PACK, P], F32, tag="turn")
            for t in range(PACK):
                nc.tensor.transpose(z_t[:, t, :], z[:, t, :], ident[:])
            z_turned[(tok, piece)] = z_t

        def scale_piece(tok, piece, on_scalar):
            stream, g = divmod(piece, PASSES)
            if g == 0:
                stream_planes = planes_pool.tile([P, PACK, PASSES, P], BF16)
                planes[(tok, stream)] = stream_planes
            z_t = z_turned[(tok, piece)]
            for t in range(PACK):
                col = PASSES * stream + g
                if on_scalar:
                    nc.scalar.activation(
                        out=planes[(tok, stream)][:, t, g, :],
                        in_=z_t[:, t, :],
                        func=ACT.Identity,
                        scale=gb_t[:, t, col : col + 1],
                        bias=gb_t[:, t, GB_ROWS + col : GB_ROWS + col + 1],
                    )
                else:
                    nc.vector.tensor_scalar(
                        out=planes[(tok, stream)][:, t, g, :],
                        in0=z_t[:, t, :],
                        scalar1=gb_t[:, t, col : col + 1],
                        scalar2=gb_t[:, t, GB_ROWS + col : GB_ROWS + col + 1],
                        op0=ALU.mult,
                        op1=ALU.add,
                    )

        def group_stream(tok, stream):
            grouped = xg_pool.tile([P, PASSES, P, PACK], BF16, align_bytes=64)
            nc.vector.tensor_copy(
                out=grouped[:].rearrange("p g k t -> p (g k) t").rearrange("p (c i) t -> p c t i", i=4),
                in_=planes[(tok, stream)][:].rearrange("p t g k -> p t (g k)").rearrange("p t (c i) -> p c t i", i=4),
            )
            x_grouped[(tok, stream)] = grouped

        def negate(tok):
            negated = xg_pool.tile([P, PASSES, P, PACK], BF16, align_bytes=64, tag="grouped")
            nc.vector.tensor_scalar(
                out=negated[:].rearrange("p g k t -> p (g k t)"),
                in0=x_grouped[(tok, IMAG)][:].rearrange("p g k t -> p (g k t)"),
                scalar1=-1.0,
                scalar2=None,
                op0=ALU.mult,
            )
            x_grouped[(tok, NEG_NI)] = negated

        acc = {}

        def multiply(tok, step, between=()):
            group, half = divmod(step, 2)
            block, kind = divmod(group, 2)
            products = (((NR, IMAG), (NI, REAL)), ((NR, REAL), (NEG_NI, IMAG)))[kind]
            last = (tok, group) == LAST_GROUP
            if half == 0 or last:
                bank = acc_psum.tile([P, N_BLOCK], F32, tag="acc")
                acc[(tok, step) if last else (tok, group)] = bank
            if last:
                cols = slice(half * N_BLOCK // 2, (half + 1) * N_BLOCK // 2)
                work = [(op, matrix, g) for op, matrix in products for g in range(PASSES)]
            else:
                cols = slice(0, N_BLOCK)
                work = [products[half] + (g,) for g in range(PASSES)]
            bank = acc[(tok, step) if last else (tok, group)]
            for i, (op, matrix, g) in enumerate(work):
                if i == len(work) // 2:
                    for piece in between:
                        turn_piece(1, piece)
                c, h = chunk_of(block, matrix, g)
                words = slice(h * N_BLOCK + cols.start, h * N_BLOCK + cols.stop)
                nc.tensor.matmul_mx(
                    out=bank[:, cols],
                    lhsT=a_codes[tok][op][:, g * P : (g + 1) * P].bitcast(FP8X4),
                    lhsT_scale=a_scales[tok][op][:, g * P : (g + 1) * P],
                    rhs=w_codes[c][:, words].bitcast(FP8X4),
                    rhs_scale=w_scales[c][:, words],
                    start=(i == 0 and (half == 0 or last)),
                    stop=(i == len(work) - 1 and (half == 1 or last)),
                )

        def store(tok, step):
            group, half = divmod(step, 2)
            block, kind = divmod(group, 2)
            part = (IMAG, REAL)[kind]
            last = (tok, group) == LAST_GROUP
            if half == 0 and not last:
                return
            cols = slice(half * N_BLOCK // 2, (half + 1) * N_BLOCK // 2) if last else slice(0, N_BLOCK)
            bank = acc[(tok, step) if last else (tok, group)]
            y = y_pool.tile([P, N_BLOCK], F32)
            nc.scalar.activation(out=y[:, cols], in_=bank[:, cols], func=ACT.Copy, scale=gain[part][:, 0:1])
            nc.sync.dma_start(
                out=outs[part][tok * P : (tok + 1) * P, block * N_BLOCK + cols.start : block * N_BLOCK + cols.stop],
                in_=y[:, cols],
            )

        def turn_and_scale(tok, pieces):
            for piece in pieces:
                turn_piece(tok, piece)
                scale_piece(tok, piece, piece in SCALAR_PIECES[tok])

        def prepare(c):
            transpose_chunk(c)
            quantise_chunk(c - 1)
            part_chunk(c + 2)

        real, imag = range(PASSES), range(PASSES, PIECES)
        statistics_on_scalar(0)
        statistics(0, V_PARTS)
        turn_gamma_and_beta()
        mean_and_rstd(0)
        for piece in real:
            centre(0, piece, nc.vector)
        transpose_chunk(0)
        turn_and_scale(0, real)
        for piece in imag:
            centre(0, piece, nc.gpsimd)
        load_x(1)
        prepare(1)
        group_stream(0, REAL)
        turn_and_scale(0, imag)
        transpose_chunk(2)
        quantise_operand(0, NR, x_grouped[(0, REAL)])
        quantise_chunk(1)
        group_stream(0, IMAG)
        transpose_chunk(3)
        quantise_operand(0, NI, x_grouped[(0, IMAG)])
        quantise_chunk(2)
        negate(0)
        quantise_operand(0, NEG_NI, x_grouped[(0, NEG_NI)])
        prepare(4)

        for step in range(STEPS + M1_LAG + 1):
            if step in TURN_STEPS_AFTER:
                for piece in TURN_STEPS_AFTER[step]:
                    scale_piece(1, piece, piece in SCALAR_PIECES[1])
            if step == 6:
                group_stream(1, REAL)
            if step == 7:
                quantise_operand(1, NR, x_grouped[(1, REAL)])
                group_stream(1, IMAG)
            if step == 8:
                quantise_operand(1, NI, x_grouped[(1, IMAG)])
                negate(1)
            if step == 9:
                quantise_operand(1, NEG_NI, x_grouped[(1, NEG_NI)])
            if step != 4:
                prepare(5 + step if step < 4 else 4 + step)
            if 0 < step <= STEPS:
                store(0, step - 1)
            if step > M1_LAG:
                store(1, step - M1_LAG - 1)
            if step < STEPS:
                multiply(0, step, TURN_STEPS.get(step, ()))
            if M1_LAG <= step < STEPS + M1_LAG:
                multiply(1, step - M1_LAG)
            if step == 0:
                statistics(1, range(4))
            if step == 1:
                statistics(1, range(4, 8), 4)
                mean_and_rstd(1)
            if step == 2:
                for piece in real:
                    centre(1, piece, nc.vector)
                for piece in imag:
                    centre(1, piece, nc.gpsimd)
